import numpy as np
import ml_dtypes


def mxq(x, axis, fmt="e4m3"):
    dtype, down = {"e4m3": (ml_dtypes.float8_e4m3fn, 7), "e5m2": (ml_dtypes.float8_e5m2, 14)}[fmt]
    v = np.moveaxis(np.asarray(x, np.float32).astype(ml_dtypes.bfloat16).astype(np.float64), axis, -1)
    blocks = v.reshape(v.shape[:-1] + (-1, 32))
    amax = np.abs(blocks).max(-1, keepdims=True)
    byte = np.maximum(np.where(amax > 0, np.frexp(amax)[1] - 1 + 127, 0) - down, 1)
    scale = np.exp2(byte - 127.0)
    codes = (blocks / scale).astype(np.float32).astype(dtype).astype(np.float64)
    return np.moveaxis((codes * scale).reshape(v.shape), -1, axis)


WIDE = False


def mx_kscale(k):
    if not WIDE:
        return np.ones(k)
    levels = np.array([10, -10, 5, -5, 0])
    a = np.random.permutation(np.resize(levels, k // 512 * 4)).reshape(k // 512, 4)
    idx = np.arange(k)
    return np.exp2(a[idx // 512, idx % 128 // 32])


BF16 = ml_dtypes.bfloat16


def bf(x):
    return np.asarray(x, np.float32).astype(BF16)


def f64(x):
    return np.asarray(x).astype(np.float64)


B, S, D_MODEL, N_HEADS, D_KV, D_ROPE = 2, 128, 5120, 8, 512, 16
D_HEAD = D_MODEL // N_HEADS
SPLIT = D_HEAD - D_ROPE
ROT_SCALE = 40.0
ROT_BASE = 10000.0


def rotate_half(x):
    x1, x2 = np.split(x, 2, axis=-1)
    return np.concatenate((-x2, x1), axis=-1)


def apply_rotary(x, cos, sin):
    r = cos.shape[-1]
    x_rot, x_base = x[..., :r], x[..., r:]
    x_rot = x_rot * cos + rotate_half(x_rot) * sin
    return np.concatenate((x_rot, x_base), axis=-1)


def rotary_emb(seq_len):
    exps = np.arange(0, D_ROPE // 2, 2, dtype=np.float64) / (D_ROPE // 2)
    inv_freq = 1.0 / ROT_BASE ** exps
    t = np.arange(seq_len, dtype=np.float64) / ROT_SCALE
    freqs = t[:, None] * inv_freq[None, :]
    return np.concatenate((freqs, freqs), axis=-1)


def setup_inputs():
    s, t = mx_kscale(D_MODEL), mx_kscale(D_KV)
    return {
        "h": bf(np.random.standard_normal((B, S, D_MODEL)) * s),
        "W_dq": bf(np.random.standard_normal((D_MODEL, D_KV)) / np.sqrt(D_MODEL) / s[:, None] * t),
        "b_dq": bf(np.random.standard_normal(D_KV) * 0.3 * t),
        "W_uq": bf(np.random.standard_normal((D_KV, N_HEADS * SPLIT)) / np.sqrt(D_KV) / t[:, None]),
        "b_uq": bf(np.random.standard_normal(N_HEADS * SPLIT) * 0.3),
        "W_qr": bf(np.random.standard_normal((D_KV, N_HEADS * D_ROPE)) * 2.0 / np.sqrt(D_KV) / t[:, None]),
        "b_qr": bf(np.random.standard_normal(N_HEADS * D_ROPE) * 0.5),
    }


def reference(h, W_dq, b_dq, W_uq, b_uq, W_qr, b_qr):
    c_q = (mxq(f64(h), 2, "e4m3") @ mxq(f64(W_dq), 0, "e4m3")) + f64(b_dq)
    cq = mxq(c_q, 2, "e4m3")
    q_base = ((cq @ mxq(f64(W_uq), 0, "e4m3")) + f64(b_uq)).reshape(B, S, N_HEADS, SPLIT)
    q_rot = ((cq @ mxq(f64(W_qr), 0, "e4m3")) + f64(b_qr)).reshape(B, S, N_HEADS, D_ROPE)
    emb = rotary_emb(S)
    cos = np.cos(emb).reshape(1, S, 1, -1)
    sin = np.sin(emb).reshape(1, S, 1, -1)
    q_rot = apply_rotary(q_rot, cos, sin)
    return np.concatenate((q_base, q_rot), axis=-1)

@@ -1,0 +1,250 @@
+from contextlib import ExitStack
+
+import concourse.masks as masks
+import concourse.mybir as mybir
+
+F32 = mybir.dt.float32
+BF16 = mybir.dt.bfloat16
+I32 = mybir.dt.int32
+U32 = mybir.dt.uint32
+U8 = mybir.dt.uint8
+FP8X4 = mybir.dt.float8_e4m3fn_x4
+ACT = mybir.ActivationFunctionType
+ALU = mybir.AluOpType
+
+P = 128
+PACK = 4
+K_PASS = P * PACK
+
+BATCH, SEQ, D_MODEL, HEADS, D_KV, D_ROPE = 2, 128, 5120, 8, 512, 16
+D_HEAD = D_MODEL // HEADS
+SPLIT = D_HEAD - D_ROPE
+ROTATED = D_ROPE // 2
+PAIRS = ROTATED // 2
+ROT_SCALE = 40.0
+ROT_BASE = 10000.0
+
+TOKENS = BATCH * SEQ
+ROUND_PASSES = 2
+ROUNDS = D_MODEL // (ROUND_PASSES * K_PASS)
+DQ_PASSES = ROUNDS * ROUND_PASSES
+KV_TILES = D_KV // P
+
+ROT_COLS = HEADS * D_ROPE
+U_COLS = ROT_COLS + HEADS * SPLIT
+GROUP = 512
+GROUPS = U_COLS // GROUP
+CHUNK_GROUPS = 2
+CHUNKS = GROUPS // CHUNK_GROUPS
+
+RUN = 4
+DQ_SCALAR_COLS = 224
+U_SCALAR_COLS = 432
+
+FLOPS = 2 * TOKENS * D_MODEL * D_KV + 2 * TOKENS * D_KV * U_COLS
+
+
+def regroup(nc, pool, rows, scalar_cols):
+    grouped = pool.tile([P, GROUP, PACK], BF16, align_bytes=64)
+    src = rows.rearrange("p t (c i) -> p c t i", i=RUN)
+    dst = grouped[:].rearrange("p (c i) t -> p c t i", i=RUN)
+    cut = scalar_cols // RUN
+    nc.scalar.copy(out=dst[:, 0:cut], in_=src[:, 0:cut])
+    nc.vector.tensor_copy(out=dst[:, cut:], in_=src[:, cut:])
+    return grouped
+
+
+def rotary_tables(nc, consts):
+    position_int = consts.tile([P, 1], I32)
+    nc.gpsimd.iota(position_int[:], pattern=[[0, 1]], base=0, channel_multiplier=1)
+    position = consts.tile([P, 1], F32)
+    nc.vector.tensor_copy(out=position[:], in_=position_int[:])
+
+    sin_half = consts.tile([P, PAIRS], F32)
+    sin_quarter = consts.tile([P, PAIRS], F32)
+    for j in range(PAIRS):
+        rate = 1.0 / (ROT_SCALE * ROT_BASE ** (j / PAIRS))
+        nc.scalar.activation(out=sin_half[:, j : j + 1], in_=position[:], func=ACT.Sin, scale=rate / 2)
+        nc.scalar.activation(out=sin_quarter[:, j : j + 1], in_=position[:], func=ACT.Sin, scale=rate / 4)
+
+    cos_half = consts.tile([P, PAIRS], F32)
+    nc.vector.tensor_tensor(out=cos_half[:], in0=sin_quarter[:], in1=sin_quarter[:], op=ALU.mult)
+    nc.vector.tensor_scalar(out=cos_half[:], in0=cos_half[:], scalar1=-2.0, scalar2=1.0, op0=ALU.mult, op1=ALU.add)
+    half_sin = consts.tile([P, PAIRS], F32)
+    nc.vector.tensor_tensor(out=half_sin[:], in0=sin_half[:], in1=cos_half[:], op=ALU.mult)
+    squared = consts.tile([P, PAIRS], F32)
+    nc.vector.tensor_tensor(out=squared[:], in0=sin_half[:], in1=sin_half[:], op=ALU.mult)
+
+    rot_cos = consts.tile([P, ROTATED], F32)
+    rot_sin = consts.tile([P, ROTATED], F32)
+    for half, sign in ((0, -2.0), (1, 2.0)):
+        cols = slice(half * PAIRS, (half + 1) * PAIRS)
+        nc.vector.tensor_scalar(out=rot_cos[:, cols], in0=squared[:], scalar1=-2.0, scalar2=1.0, op0=ALU.mult, op1=ALU.add)
+        nc.vector.tensor_scalar_mul(out=rot_sin[:, cols], in0=half_sin[:], scalar1=sign)
+    return rot_cos, rot_sin
+
+
+def rotate(nc, pool, q_rot, rot_cos, rot_sin):
+    straight = pool.tile([P, HEADS, ROTATED], F32)
+    crossed = pool.tile([P, HEADS, ROTATED], F32)
+    low, high = slice(0, PAIRS), slice(PAIRS, ROTATED)
+    nc.vector.tensor_tensor(
+        out=straight[:], in0=q_rot[:, :, 0:ROTATED],
+        in1=rot_cos[:].unsqueeze(1).to_broadcast([P, HEADS, ROTATED]), op=ALU.mult,
+    )
+    for here, there in ((low, high), (high, low)):
+        nc.vector.tensor_tensor(
+            out=crossed[:, :, here], in0=q_rot[:, :, there],
+            in1=rot_sin[:, here].unsqueeze(1).to_broadcast([P, HEADS, PAIRS]), op=ALU.mult,
+        )
+    nc.vector.tensor_tensor(out=q_rot[:, :, 0:ROTATED], in0=straight[:], in1=crossed[:], op=ALU.add)
+
+
+def tile_mla_pa_kernel(tc, h, W_dq, b_dq, W_uq, b_uq, W_qr, b_qr, out):
+    nc = tc.nc
+    with ExitStack() as ctx:
+        consts = ctx.enter_context(tc.tile_pool(name="consts", bufs=1))
+        keep = ctx.enter_context(tc.tile_pool(name="keep", bufs=1))
+        h_raw = ctx.enter_context(tc.tile_pool(name="h_raw", bufs=ROUNDS))
+        dq_raw = ctx.enter_context(tc.tile_pool(name="dq_raw", bufs=ROUNDS))
+        u_raw = ctx.enter_context(tc.tile_pool(name="u_raw", bufs=3))
+        h_stage = ctx.enter_context(tc.tile_pool(name="h_stage", bufs=3))
+        w_stage = ctx.enter_context(tc.tile_pool(name="w_stage", bufs=4))
+        rot_stage = ctx.enter_context(tc.tile_pool(name="rot_stage", bufs=2))
+        accs = ctx.enter_context(tc.psum_pool(name="accs", bufs=1))
+        banks = ctx.enter_context(tc.psum_pool(name="banks", bufs=4))
+
+        identity = consts.tile([P, P], F32)
+        masks.make_identity(nc, identity[:])
+        rot_cos, rot_sin = rotary_tables(nc, consts)
+
+        h_codes = keep.tile([P, DQ_PASSES, TOKENS], U32, align_bytes=64)
+        h_scales = keep.tile([P, DQ_PASSES, TOKENS], U8, align_bytes=64)
+        dq_codes = keep.tile([P, DQ_PASSES, D_KV], U32, align_bytes=64)
+        dq_scales = keep.tile([P, DQ_PASSES, D_KV], U8, align_bytes=64)
+        acc = [accs.tile([P, TOKENS], F32, name="acc%d" % m) for m in range(KV_TILES)]
+
+        round_k = ROUND_PASSES * K_PASS
+        for r in range(ROUNDS):
+            k_range = slice(r * round_k, (r + 1) * round_k)
+            h_rows = h_raw.tile([P, BATCH, round_k], BF16)
+            nc.sync.dma_start(out=h_rows[:], in_=h[:, :, k_range].rearrange("b s k -> s b k"))
+            dq_rows = dq_raw.tile([P, ROUND_PASSES, PACK, D_KV], BF16)
+            nc.sync.dma_start(
+                out=dq_rows[:], in_=W_dq[k_range, :].rearrange("(g p t) c -> p g t c", p=P, t=PACK)
+            )
+            h_words = h_rows[:].bitcast(F32).rearrange("s b (g p u) -> s b g u p", p=P, u=2)
+
+            for i in range(ROUND_PASSES):
+                g = r * ROUND_PASSES + i
+                turned = banks.tile([P, 2, TOKENS], F32, tag="bank")
+                for b in range(BATCH):
+                    for u in range(2):
+                        nc.tensor.transpose(
+                            out=turned[:, u, b * SEQ : (b + 1) * SEQ],
+                            in_=h_words[:, b, i, u, :],
+                            identity=identity[:],
+                        )
+                h_grouped = h_stage.tile([P, TOKENS * PACK], BF16, align_bytes=64)
+                nc.scalar.copy(
+                    out=h_grouped[:].bitcast(F32).rearrange("p (s u) -> p s u", u=2),
+                    in_=turned[:].rearrange("p u s -> p s u"),
+                )
+                nc.vector.quantize_mx(
+                    out=h_codes[:, g, :].bitcast(FP8X4), scales=h_scales[:, g, :], in_=h_grouped[:]
+                )
+
+                dq_grouped = regroup(nc, w_stage, dq_rows[:, i], DQ_SCALAR_COLS)
+                nc.vector.quantize_mx(
+                    out=dq_codes[:, g, :].bitcast(FP8X4),
+                    scales=dq_scales[:, g, :],
+                    in_=dq_grouped[:].rearrange("p c t -> p (c t)"),
+                )
+                for m in range(KV_TILES):
+                    cols = slice(m * P, (m + 1) * P)
+                    nc.tensor.matmul_mx(
+                        out=acc[m][:],
+                        lhsT=dq_codes[:, g, cols].bitcast(FP8X4),
+                        lhsT_scale=dq_scales[:, g, cols],
+                        rhs=h_codes[:, g, :].bitcast(FP8X4),
+                        rhs_scale=h_scales[:, g, :],
+                        start=(g == 0),
+                        stop=(g == DQ_PASSES - 1),
+                    )
+
+        b_dq_bf = consts.tile([P, KV_TILES], BF16)
+        with nc.allow_non_contiguous_dma(reason="512 bias values, one to a partition and tile"):
+            nc.sync.dma_start(out=b_dq_bf[:], in_=b_dq.rearrange("(m p) -> p m", p=P))
+        b_dq_col = consts.tile([P, KV_TILES], F32)
+        nc.vector.tensor_copy(out=b_dq_col[:], in_=b_dq_bf[:])
+
+        cq_rows = keep.tile([P, KV_TILES, TOKENS], BF16)
+        for m in range(KV_TILES):
+            if m % 2 == 0:
+                nc.scalar.activation(
+                    out=cq_rows[:, m, :], in_=acc[m][:], func=ACT.Identity, bias=b_dq_col[:, m : m + 1]
+                )
+            else:
+                nc.vector.tensor_scalar_add(out=cq_rows[:, m, :], in0=acc[m][:], scalar1=b_dq_col[:, m : m + 1])
+        cq_grouped = keep.tile([P, TOKENS, PACK], BF16, align_bytes=64)
+        nc.vector.tensor_copy(
+            out=cq_grouped[:].rearrange("p (c i) t -> p c t i", i=RUN),
+            in_=cq_rows[:].rearrange("p t (c i) -> p c t i", i=RUN),
+        )
+        cq_codes = keep.tile([P, TOKENS], U32, align_bytes=64)
+        cq_scales = keep.tile([P, TOKENS], U8, align_bytes=64)
+        nc.vector.quantize_mx(
+            out=cq_codes[:].bitcast(FP8X4), scales=cq_scales[:], in_=cq_grouped[:].rearrange("p c t -> p (c t)")
+        )
+
+        bias = keep.tile([P, U_COLS], BF16)
+        nc.sync.dma_start(out=bias[:, 0:ROT_COLS], in_=b_qr.partition_broadcast(P))
+        nc.sync.dma_start(out=bias[:, ROT_COLS:U_COLS], in_=b_uq.partition_broadcast(P))
+
+        u_codes = keep.tile([P, GROUPS, GROUP], U32, align_bytes=64)
+        u_scales = keep.tile([P, GROUPS, GROUP], U8, align_bytes=64)
+        result = [keep.tile([P, U_COLS], F32, name="result%d" % b) for b in range(BATCH)]
+        qr_rows = W_qr.rearrange("(t p) c -> p t c", p=P)
+        uq_rows = W_uq.rearrange("(t p) c -> p t c", p=P)
+        chunk_cols = CHUNK_GROUPS * GROUP
+
+        for j in range(CHUNKS):
+            u_rows = u_raw.tile([P, PACK, chunk_cols], BF16)
+            if j == 0:
+                nc.sync.dma_start(out=u_rows[:, :, 0:ROT_COLS], in_=qr_rows)
+                nc.sync.dma_start(out=u_rows[:, :, ROT_COLS:chunk_cols], in_=uq_rows[:, :, 0 : chunk_cols - ROT_COLS])
+            else:
+                first = j * chunk_cols - ROT_COLS
+                nc.sync.dma_start(out=u_rows[:], in_=uq_rows[:, :, first : first + chunk_cols])
+
+            for i in range(CHUNK_GROUPS):
+                n = j * CHUNK_GROUPS + i
+                cols = slice(n * GROUP, (n + 1) * GROUP)
+                u_grouped = regroup(nc, w_stage, u_rows[:, :, i * GROUP : (i + 1) * GROUP], U_SCALAR_COLS)
+                nc.vector.quantize_mx(
+                    out=u_codes[:, n, :].bitcast(FP8X4),
+                    scales=u_scales[:, n, :],
+                    in_=u_grouped[:].rearrange("p c t -> p (c t)"),
+                )
+                for b in range(BATCH):
+                    tokens = slice(b * SEQ, (b + 1) * SEQ)
+                    product = banks.tile([P, GROUP], F32, tag="bank")
+                    nc.tensor.matmul_mx(
+                        out=product[:],
+                        lhsT=cq_codes[:, tokens].bitcast(FP8X4),
+                        lhsT_scale=cq_scales[:, tokens],
+                        rhs=u_codes[:, n, :].bitcast(FP8X4),
+                        rhs_scale=u_scales[:, n, :],
+                        start=True,
+                        stop=True,
+                    )
+                    nc.vector.tensor_tensor(out=result[b][:, cols], in0=product[:], in1=bias[:, cols], op=ALU.add)
+
+                    if n == 0:
+                        q_rot = result[b][:, 0:ROT_COLS].rearrange("p (a d) -> p a d", d=D_ROPE)
+                        rotate(nc, rot_stage, q_rot, rot_cos, rot_sin)
+                        nc.sync.dma_start(out=out[b, :, :, SPLIT:D_HEAD], in_=q_rot)
+                    for a in range(HEADS):
+                        first = ROT_COLS + a * SPLIT
+                        if (first + SPLIT - 1) // GROUP == n:
+                            nc.sync.dma_start(out=out[b, :, a, 0:SPLIT], in_=result[b][:, first : first + SPLIT])

@@ -41,6 +41,9 @@ RUN = 4
 DQ_SCALAR_COLS = 224
 U_SCALAR_COLS = 432
 
+W_STAGE_BUFS = 4
+TURN_AHEAD = 2
+
 FLOPS = 2 * TOKENS * D_MODEL * D_KV + 2 * TOKENS * D_KV * U_COLS
 
 
@@ -84,81 +87,116 @@ def rotary_tables(nc, consts):
     return rot_cos, rot_sin
 
 
-def rotate(nc, pool, q_rot, rot_cos, rot_sin):
-    straight = pool.tile([P, HEADS, ROTATED], F32)
-    crossed = pool.tile([P, HEADS, ROTATED], F32)
+def rotate(nc, pool, q_rots, rot_cos, rot_sin):
     low, high = slice(0, PAIRS), slice(PAIRS, ROTATED)
-    nc.vector.tensor_tensor(
-        out=straight[:], in0=q_rot[:, :, 0:ROTATED],
-        in1=rot_cos[:].unsqueeze(1).to_broadcast([P, HEADS, ROTATED]), op=ALU.mult,
-    )
-    for here, there in ((low, high), (high, low)):
+    straight = [pool.tile([P, HEADS, ROTATED], F32, name="straight%d" % b) for b in range(BATCH)]
+    crossed = [pool.tile([P, HEADS, ROTATED], F32, name="crossed%d" % b) for b in range(BATCH)]
+    for b in range(BATCH):
         nc.vector.tensor_tensor(
-            out=crossed[:, :, here], in0=q_rot[:, :, there],
-            in1=rot_sin[:, here].unsqueeze(1).to_broadcast([P, HEADS, PAIRS]), op=ALU.mult,
+            out=straight[b][:], in0=q_rots[b][:, :, 0:ROTATED],
+            in1=rot_cos[:].unsqueeze(1).to_broadcast([P, HEADS, ROTATED]), op=ALU.mult,
         )
-    nc.vector.tensor_tensor(out=q_rot[:, :, 0:ROTATED], in0=straight[:], in1=crossed[:], op=ALU.add)
+    for here, there in ((low, high), (high, low)):
+        for b in range(BATCH):
+            nc.vector.tensor_tensor(
+                out=crossed[b][:, :, here], in0=q_rots[b][:, :, there],
+                in1=rot_sin[:, here].unsqueeze(1).to_broadcast([P, HEADS, PAIRS]), op=ALU.mult,
+            )
+    for b in range(BATCH):
+        nc.vector.tensor_tensor(
+            out=q_rots[b][:, :, 0:ROTATED], in0=straight[b][:], in1=crossed[b][:], op=ALU.add
+        )
 
 
 def tile_mla_pa_kernel(tc, h, W_dq, b_dq, W_uq, b_uq, W_qr, b_qr, out):
     nc = tc.nc
     with ExitStack() as ctx:
+        ctx.enter_context(tc.manual_schedule())
         consts = ctx.enter_context(tc.tile_pool(name="consts", bufs=1))
         keep = ctx.enter_context(tc.tile_pool(name="keep", bufs=1))
-        h_raw = ctx.enter_context(tc.tile_pool(name="h_raw", bufs=ROUNDS))
-        dq_raw = ctx.enter_context(tc.tile_pool(name="dq_raw", bufs=ROUNDS))
-        u_raw = ctx.enter_context(tc.tile_pool(name="u_raw", bufs=3))
         h_stage = ctx.enter_context(tc.tile_pool(name="h_stage", bufs=3))
-        w_stage = ctx.enter_context(tc.tile_pool(name="w_stage", bufs=4))
-        rot_stage = ctx.enter_context(tc.tile_pool(name="rot_stage", bufs=2))
+        w_stage = ctx.enter_context(tc.tile_pool(name="w_stage", bufs=W_STAGE_BUFS))
         accs = ctx.enter_context(tc.psum_pool(name="accs", bufs=1))
         banks = ctx.enter_context(tc.psum_pool(name="banks", bufs=4))
 
-        identity = consts.tile([P, P], F32)
-        masks.make_identity(nc, identity[:])
-        rot_cos, rot_sin = rotary_tables(nc, consts)
+        cq_codes = keep.tile([P, TOKENS], U32, align_bytes=64)
+        cq_scales = keep.tile([P, TOKENS], U8, align_bytes=64)
+        bias = keep.tile([P, U_COLS], BF16)
+        u_codes = keep.tile([P, GROUPS, GROUP], U32, align_bytes=64)
+        u_scales = keep.tile([P, GROUPS, GROUP], U8, align_bytes=64)
+        chunk_cols = CHUNK_GROUPS * GROUP
+        u_rows = [keep.tile([P, PACK, chunk_cols], BF16, name="u_rows%d" % j) for j in range(CHUNKS)]
 
-        h_codes = keep.tile([P, DQ_PASSES, TOKENS], U32, align_bytes=64)
-        h_scales = keep.tile([P, DQ_PASSES, TOKENS], U8, align_bytes=64)
-        dq_codes = keep.tile([P, DQ_PASSES, D_KV], U32, align_bytes=64)
-        dq_scales = keep.tile([P, DQ_PASSES, D_KV], U8, align_bytes=64)
-        acc = [accs.tile([P, TOKENS], F32, name="acc%d" % m) for m in range(KV_TILES)]
+        with tc.tile_pool(name="first", bufs=1) as first:
+            round_k = ROUND_PASSES * K_PASS
+            h_rows = [first.tile([P, BATCH, round_k], BF16, name="h_rows%d" % r) for r in range(ROUNDS)]
+            dq_rows = [first.tile([P, PACK, D_KV], BF16, name="dq_rows%d" % g) for g in range(DQ_PASSES)]
+            h_codes = first.tile([P, DQ_PASSES, TOKENS], U32, align_bytes=64)
+            h_scales = first.tile([P, DQ_PASSES, TOKENS], U8, align_bytes=64)
+            dq_codes = first.tile([P, DQ_PASSES, D_KV], U32, align_bytes=64)
+            dq_scales = first.tile([P, DQ_PASSES, D_KV], U8, align_bytes=64)
+            acc = [accs.tile([P, TOKENS], F32, name="acc%d" % m) for m in range(KV_TILES)]
 
-        round_k = ROUND_PASSES * K_PASS
-        for r in range(ROUNDS):
-            k_range = slice(r * round_k, (r + 1) * round_k)
-            h_rows = h_raw.tile([P, BATCH, round_k], BF16)
-            nc.sync.dma_start(out=h_rows[:], in_=h[:, :, k_range].rearrange("b s k -> s b k"))
-            dq_rows = dq_raw.tile([P, ROUND_PASSES, PACK, D_KV], BF16)
-            nc.sync.dma_start(
-                out=dq_rows[:], in_=W_dq[k_range, :].rearrange("(g p t) c -> p g t c", p=P, t=PACK)
-            )
-            h_words = h_rows[:].bitcast(F32).rearrange("s b (g p u) -> s b g u p", p=P, u=2)
+            ones = first.tile([P, P], BF16)
+            bias_row = first.tile([P, U_COLS], BF16)
+            nc.vector.memset(bias_row[:].bitcast(I32), 0)
+            nc.vector.memset(ones[:], 1.0)
+            nc.scalar.dma_start(out=bias_row[0:1, 0:ROT_COLS], in_=b_qr.unsqueeze(0))
+            nc.scalar.dma_start(out=bias_row[0:1, ROT_COLS:U_COLS], in_=b_uq.unsqueeze(0))
 
-            for i in range(ROUND_PASSES):
-                g = r * ROUND_PASSES + i
-                turned = banks.tile([P, 2, TOKENS], F32, tag="bank")
+            b_dq_bf = consts.tile([P, KV_TILES], BF16)
+            with nc.allow_non_contiguous_dma(reason="512 bias values, one to a partition and tile"):
+                nc.scalar.dma_start(out=b_dq_bf[:], in_=b_dq.rearrange("(m p) -> p m", p=P))
+
+            for r in range(ROUNDS):
+                k_range = slice(r * round_k, (r + 1) * round_k)
+                nc.sync.dma_start(out=h_rows[r][:], in_=h[:, :, k_range].rearrange("b s k -> s b k"))
+                for g in range(r * ROUND_PASSES, (r + 1) * ROUND_PASSES):
+                    nc.sync.dma_start(
+                        out=dq_rows[g][:],
+                        in_=W_dq[g * K_PASS : (g + 1) * K_PASS, :].rearrange("(p t) c -> p t c", t=PACK),
+                    )
+            qr_rows = W_qr.rearrange("(t p) c -> p t c", p=P)
+            uq_rows = W_uq.rearrange("(t p) c -> p t c", p=P)
+            nc.sync.dma_start(out=u_rows[0][:, :, 0:ROT_COLS], in_=qr_rows)
+            nc.sync.dma_start(out=u_rows[0][:, :, ROT_COLS:chunk_cols], in_=uq_rows[:, :, 0 : chunk_cols - ROT_COLS])
+            for j in range(1, CHUNKS):
+                start_col = j * chunk_cols - ROT_COLS
+                nc.sync.dma_start(out=u_rows[j][:], in_=uq_rows[:, :, start_col : start_col + chunk_cols])
+
+            identity = consts.tile([P, P], F32)
+            masks.make_identity(nc, identity[:])
+            rot_cos, rot_sin = rotary_tables(nc, consts)
+            b_dq_col = consts.tile([P, KV_TILES], F32)
+
+            turned, h_grouped, dq_grouped = {}, {}, {}
+
+            def turn(g):
+                r, i = divmod(g, ROUND_PASSES)
+                words = h_rows[r][:].bitcast(F32).rearrange("s b (g p u) -> s b g u p", p=P, u=2)
+                turned[g] = banks.tile([P, 2, TOKENS], F32, tag="bank", name="turned")
                 for b in range(BATCH):
                     for u in range(2):
                         nc.tensor.transpose(
-                            out=turned[:, u, b * SEQ : (b + 1) * SEQ],
-                            in_=h_words[:, b, i, u, :],
-                            identity=identity[:],
+                            out=turned[g][:, u, b * SEQ : (b + 1) * SEQ], in_=words[:, b, i, u, :], identity=identity[:]
                         )
-                h_grouped = h_stage.tile([P, TOKENS * PACK], BF16, align_bytes=64)
-                nc.scalar.copy(
-                    out=h_grouped[:].bitcast(F32).rearrange("p (s u) -> p s u", u=2),
-                    in_=turned[:].rearrange("p u s -> p s u"),
-                )
-                nc.vector.quantize_mx(
-                    out=h_codes[:, g, :].bitcast(FP8X4), scales=h_scales[:, g, :], in_=h_grouped[:]
-                )
 
-                dq_grouped = regroup(nc, w_stage, dq_rows[:, i], DQ_SCALAR_COLS)
+            def group_first(g):
+                h_grouped[g] = h_stage.tile([P, TOKENS * PACK], BF16, align_bytes=64, name="h_grouped")
+                nc.scalar.copy(
+                    out=h_grouped[g][:].bitcast(F32).rearrange("p (s u) -> p s u", u=2),
+                    in_=turned[g][:].rearrange("p u s -> p s u"),
+                )
+                dq_grouped[g] = regroup(nc, w_stage, dq_rows[g][:], DQ_SCALAR_COLS)
+
+            def multiply_first(g):
+                nc.vector.quantize_mx(
+                    out=h_codes[:, g, :].bitcast(FP8X4), scales=h_scales[:, g, :], in_=h_grouped[g][:]
+                )
                 nc.vector.quantize_mx(
                     out=dq_codes[:, g, :].bitcast(FP8X4),
                     scales=dq_scales[:, g, :],
-                    in_=dq_grouped[:].rearrange("p c t -> p (c t)"),
+                    in_=dq_grouped[g][:].rearrange("p c t -> p (c t)"),
                 )
                 for m in range(KV_TILES):
                     cols = slice(m * P, (m + 1) * P)
@@ -172,65 +210,33 @@ def tile_mla_pa_kernel(tc, h, W_dq, b_dq, W_uq, b_uq, W_qr, b_qr, out):
                         stop=(g == DQ_PASSES - 1),
                     )
 
-        b_dq_bf = consts.tile([P, KV_TILES], BF16)
-        with nc.allow_non_contiguous_dma(reason="512 bias values, one to a partition and tile"):
-            nc.sync.dma_start(out=b_dq_bf[:], in_=b_dq.rearrange("(m p) -> p m", p=P))
-        b_dq_col = consts.tile([P, KV_TILES], F32)
-        nc.vector.tensor_copy(out=b_dq_col[:], in_=b_dq_bf[:])
+            for g in range(TURN_AHEAD):
+                turn(g)
+            for step in range(DQ_PASSES + 1):
+                if step + TURN_AHEAD < DQ_PASSES:
+                    turn(step + TURN_AHEAD)
+                if step < DQ_PASSES:
+                    group_first(step)
+                if step >= 1:
+                    multiply_first(step - 1)
 
-        cq_rows = keep.tile([P, KV_TILES, TOKENS], BF16)
-        for m in range(KV_TILES):
-            if m % 2 == 0:
-                nc.scalar.activation(
-                    out=cq_rows[:, m, :], in_=acc[m][:], func=ACT.Identity, bias=b_dq_col[:, m : m + 1]
-                )
-            else:
-                nc.vector.tensor_scalar_add(out=cq_rows[:, m, :], in0=acc[m][:], scalar1=b_dq_col[:, m : m + 1])
-        cq_grouped = keep.tile([P, TOKENS, PACK], BF16, align_bytes=64)
-        nc.vector.tensor_copy(
-            out=cq_grouped[:].rearrange("p (c i) t -> p c t i", i=RUN),
-            in_=cq_rows[:].rearrange("p t (c i) -> p c t i", i=RUN),
-        )
-        cq_codes = keep.tile([P, TOKENS], U32, align_bytes=64)
-        cq_scales = keep.tile([P, TOKENS], U8, align_bytes=64)
-        nc.vector.quantize_mx(
-            out=cq_codes[:].bitcast(FP8X4), scales=cq_scales[:], in_=cq_grouped[:].rearrange("p c t -> p (c t)")
-        )
+            u_grouped, product = {}, {}
 
-        bias = keep.tile([P, U_COLS], BF16)
-        nc.sync.dma_start(out=bias[:, 0:ROT_COLS], in_=b_qr.partition_broadcast(P))
-        nc.sync.dma_start(out=bias[:, ROT_COLS:U_COLS], in_=b_uq.partition_broadcast(P))
+            def group_second(n):
+                j, i = divmod(n, CHUNK_GROUPS)
+                u_grouped[n] = regroup(nc, w_stage, u_rows[j][:, :, i * GROUP : (i + 1) * GROUP], U_SCALAR_COLS)
 
-        u_codes = keep.tile([P, GROUPS, GROUP], U32, align_bytes=64)
-        u_scales = keep.tile([P, GROUPS, GROUP], U8, align_bytes=64)
-        result = [keep.tile([P, U_COLS], F32, name="result%d" % b) for b in range(BATCH)]
-        qr_rows = W_qr.rearrange("(t p) c -> p t c", p=P)
-        uq_rows = W_uq.rearrange("(t p) c -> p t c", p=P)
-        chunk_cols = CHUNK_GROUPS * GROUP
-
-        for j in range(CHUNKS):
-            u_rows = u_raw.tile([P, PACK, chunk_cols], BF16)
-            if j == 0:
-                nc.sync.dma_start(out=u_rows[:, :, 0:ROT_COLS], in_=qr_rows)
-                nc.sync.dma_start(out=u_rows[:, :, ROT_COLS:chunk_cols], in_=uq_rows[:, :, 0 : chunk_cols - ROT_COLS])
-            else:
-                first = j * chunk_cols - ROT_COLS
-                nc.sync.dma_start(out=u_rows[:], in_=uq_rows[:, :, first : first + chunk_cols])
-
-            for i in range(CHUNK_GROUPS):
-                n = j * CHUNK_GROUPS + i
-                cols = slice(n * GROUP, (n + 1) * GROUP)
-                u_grouped = regroup(nc, w_stage, u_rows[:, :, i * GROUP : (i + 1) * GROUP], U_SCALAR_COLS)
+            def multiply_second(n):
                 nc.vector.quantize_mx(
                     out=u_codes[:, n, :].bitcast(FP8X4),
                     scales=u_scales[:, n, :],
-                    in_=u_grouped[:].rearrange("p c t -> p (c t)"),
+                    in_=u_grouped[n][:].rearrange("p c t -> p (c t)"),
                 )
                 for b in range(BATCH):
                     tokens = slice(b * SEQ, (b + 1) * SEQ)
-                    product = banks.tile([P, GROUP], F32, tag="bank")
+                    product[n, b] = banks.tile([P, GROUP], F32, tag="bank", name="product")
                     nc.tensor.matmul_mx(
-                        out=product[:],
+                        out=product[n, b][:],
                         lhsT=cq_codes[:, tokens].bitcast(FP8X4),
                         lhsT_scale=cq_scales[:, tokens],
                         rhs=u_codes[:, n, :].bitcast(FP8X4),
@@ -238,13 +244,74 @@ def tile_mla_pa_kernel(tc, h, W_dq, b_dq, W_uq, b_uq, W_qr, b_qr, out):
                         start=True,
                         stop=True,
                     )
-                    nc.vector.tensor_tensor(out=result[b][:, cols], in0=product[:], in1=bias[:, cols], op=ALU.add)
 
-                    if n == 0:
-                        q_rot = result[b][:, 0:ROT_COLS].rearrange("p (a d) -> p a d", d=D_ROPE)
-                        rotate(nc, rot_stage, q_rot, rot_cos, rot_sin)
-                        nc.sync.dma_start(out=out[b, :, :, SPLIT:D_HEAD], in_=q_rot)
-                    for a in range(HEADS):
-                        first = ROT_COLS + a * SPLIT
-                        if (first + SPLIT - 1) // GROUP == n:
-                            nc.sync.dma_start(out=out[b, :, a, 0:SPLIT], in_=result[b][:, first : first + SPLIT])
+            def spread_bias(pair):
+                spread = banks.tile([P, 2 * GROUP], BF16, tag="bank")
+                for i in range(2):
+                    start_col = (2 * pair + i) * GROUP
+                    nc.tensor.matmul(
+                        out=spread[:, i * GROUP : (i + 1) * GROUP],
+                        lhsT=ones[:],
+                        rhs=bias_row[:, start_col : start_col + GROUP],
+                        start=True,
+                        stop=True,
+                    )
+                cols = slice(2 * pair * GROUP, 2 * (pair + 1) * GROUP)
+                if pair % 2 == 0:
+                    nc.scalar.copy(out=bias[:, cols], in_=spread[:])
+                else:
+                    nc.vector.tensor_copy(out=bias[:, cols], in_=spread[:])
+
+            group_second(0)
+            nc.vector.tensor_copy(out=b_dq_col[:], in_=b_dq_bf[:])
+            cq_rows = first.tile([P, KV_TILES, TOKENS], BF16)
+            for m in range(KV_TILES):
+                if m % 2 == 0:
+                    nc.scalar.activation(
+                        out=cq_rows[:, m, :], in_=acc[m][:], func=ACT.Identity, bias=b_dq_col[:, m : m + 1]
+                    )
+                else:
+                    nc.vector.tensor_scalar_add(
+                        out=cq_rows[:, m, :], in0=acc[m][:], scalar1=b_dq_col[:, m : m + 1]
+                    )
+            spread_bias(0)
+            spread_bias(1)
+            cq_grouped = first.tile([P, TOKENS, PACK], BF16, align_bytes=64)
+            nc.vector.tensor_copy(
+                out=cq_grouped[:].rearrange("p (c i) t -> p c t i", i=RUN),
+                in_=cq_rows[:].rearrange("p t (c i) -> p c t i", i=RUN),
+            )
+            group_second(1)
+            nc.vector.quantize_mx(
+                out=cq_codes[:].bitcast(FP8X4),
+                scales=cq_scales[:],
+                in_=cq_grouped[:].rearrange("p c t -> p (c t)"),
+            )
+            for pair in range(2, GROUPS // 2):
+                spread_bias(pair)
+            multiply_second(0)
+
+        results = ctx.enter_context(tc.tile_pool(name="results", bufs=1))
+        result = [results.tile([P, U_COLS], F32, name="result%d" % b) for b in range(BATCH)]
+
+        def leave_second(n):
+            cols = slice(n * GROUP, (n + 1) * GROUP)
+            for b in range(BATCH):
+                nc.vector.tensor_tensor(out=result[b][:, cols], in0=product[n, b][:], in1=bias[:, cols], op=ALU.add)
+            if n == 0:
+                q_rots = [result[b][:, 0:ROT_COLS].rearrange("p (a d) -> p a d", d=D_ROPE) for b in range(BATCH)]
+                rotate(nc, results, q_rots, rot_cos, rot_sin)
+                for b in range(BATCH):
+                    nc.sync.dma_start(out=out[b, :, :, SPLIT:D_HEAD], in_=q_rots[b])
+            for a in range(HEADS):
+                start_col = ROT_COLS + a * SPLIT
+                if (start_col + SPLIT - 1) // GROUP == n:
+                    for b in range(BATCH):
+                        nc.sync.dma_start(out=out[b, :, a, 0:SPLIT], in_=result[b][:, start_col : start_col + SPLIT])
+
+        for step in range(2, GROUPS + 2):
+            if step < GROUPS:
+                group_second(step)
+            if step - 1 < GROUPS:
+                multiply_second(step - 1)
+            leave_second(step - 2)

@@ -40,20 +40,27 @@ CHUNKS = GROUPS // CHUNK_GROUPS
 RUN = 4
 DQ_SCALAR_COLS = 224
 U_SCALAR_COLS = 432
+GPSIMD_FROM = W_STAGE_BUFS = 4
+U_GPSIMD_COLS = 128
 
-W_STAGE_BUFS = 4
 TURN_AHEAD = 2
 
 FLOPS = 2 * TOKENS * D_MODEL * D_KV + 2 * TOKENS * D_KV * U_COLS
 
 
-def regroup(nc, pool, rows, scalar_cols):
+def regroup(nc, pool, rows, scalar_cols, gpsimd=False):
     grouped = pool.tile([P, GROUP, PACK], BF16, align_bytes=64)
     src = rows.rearrange("p t (c i) -> p c t i", i=RUN)
     dst = grouped[:].rearrange("p (c i) t -> p c t i", i=RUN)
     cut = scalar_cols // RUN
     nc.scalar.copy(out=dst[:, 0:cut], in_=src[:, 0:cut])
-    nc.vector.tensor_copy(out=dst[:, cut:], in_=src[:, cut:])
+    if gpsimd:
+        nc.gpsimd.tensor_scalar(
+            out=grouped[:, scalar_cols:, :], in0=rows[:, :, scalar_cols:].rearrange("p t c -> p c t"),
+            scalar1=1.0, scalar2=0.0, op0=ALU.mult, op1=ALU.add,
+        )
+    else:
+        nc.vector.tensor_copy(out=dst[:, cut:], in_=src[:, cut:])
     return grouped
 
 
@@ -224,7 +231,11 @@ def tile_mla_pa_kernel(tc, h, W_dq, b_dq, W_uq, b_uq, W_qr, b_qr, out):
 
             def group_second(n):
                 j, i = divmod(n, CHUNK_GROUPS)
-                u_grouped[n] = regroup(nc, w_stage, u_rows[j][:, :, i * GROUP : (i + 1) * GROUP], U_SCALAR_COLS)
+                u_cols = u_rows[j][:, :, i * GROUP : (i + 1) * GROUP]
+                if n >= GPSIMD_FROM:
+                    u_grouped[n] = regroup(nc, w_stage, u_cols, GROUP - U_GPSIMD_COLS, gpsimd=True)
+                else:
+                    u_grouped[n] = regroup(nc, w_stage, u_cols, U_SCALAR_COLS)
 
             def multiply_second(n):
                 nc.vector.quantize_mx(

@@ -37,7 +37,7 @@ GROUPS = U_COLS // GROUP
 CHUNK_GROUPS = 2
 CHUNKS = GROUPS // CHUNK_GROUPS
 
-RUN = 4
+RUN = 8
 DQ_SCALAR_COLS = 224
 U_SCALAR_COLS = 432
 GPSIMD_FROM = W_STAGE_BUFS = 4

@@ -144,25 +144,36 @@ def tile_mla_pa_kernel(tc, h, W_dq, b_dq, W_uq, b_uq, W_qr, b_qr, out):
             dq_scales = first.tile([P, DQ_PASSES, D_KV], U8, align_bytes=64)
             acc = [accs.tile([P, TOKENS], F32, name="acc%d" % m) for m in range(KV_TILES)]
 
-            ones = first.tile([P, P], BF16)
-            bias_row = first.tile([P, U_COLS], BF16)
-            nc.vector.memset(bias_row[:].bitcast(I32), 0)
-            nc.vector.memset(ones[:], 1.0)
-            nc.scalar.dma_start(out=bias_row[0:1, 0:ROT_COLS], in_=b_qr.unsqueeze(0))
-            nc.scalar.dma_start(out=bias_row[0:1, ROT_COLS:U_COLS], in_=b_uq.unsqueeze(0))
+            bias_rows = first.tile([P, GROUP], BF16)
+            nc.vector.memset(bias_rows[:].bitcast(I32), 0)
+            rot_cos, rot_sin = rotary_tables(nc, consts)
+            identity = consts.tile([P, P], F32)
+            masks.make_identity(nc, identity[:])
+            identity_bf = consts.tile([P, P], BF16)
+            masks.make_identity(nc, identity_bf[:])
+            first_cols = GROUP - ROT_COLS
+            nc.gpsimd.dma_start(out=bias_rows[0:1, 0:ROT_COLS], in_=b_qr.unsqueeze(0))
+            nc.gpsimd.dma_start(out=bias_rows[0:1, ROT_COLS:GROUP], in_=b_uq[0:first_cols].unsqueeze(0))
+            nc.gpsimd.dma_start(
+                out=bias_rows[1:GROUPS, :], in_=b_uq[first_cols:].rearrange("(n c) -> n c", c=GROUP)
+            )
 
             b_dq_bf = consts.tile([P, KV_TILES], BF16)
             with nc.allow_non_contiguous_dma(reason="512 bias values, one to a partition and tile"):
-                nc.scalar.dma_start(out=b_dq_bf[:], in_=b_dq.rearrange("(m p) -> p m", p=P))
+                nc.gpsimd.dma_start(out=b_dq_bf[:], in_=b_dq.rearrange("(m p) -> p m", p=P))
 
+            def load_dq(g):
+                nc.sync.dma_start(
+                    out=dq_rows[g][:],
+                    in_=W_dq[g * K_PASS : (g + 1) * K_PASS, :].rearrange("(p t) c -> p t c", t=PACK),
+                )
+
+            load_dq(0)
             for r in range(ROUNDS):
                 k_range = slice(r * round_k, (r + 1) * round_k)
                 nc.sync.dma_start(out=h_rows[r][:], in_=h[:, :, k_range].rearrange("b s k -> s b k"))
-                for g in range(r * ROUND_PASSES, (r + 1) * ROUND_PASSES):
-                    nc.sync.dma_start(
-                        out=dq_rows[g][:],
-                        in_=W_dq[g * K_PASS : (g + 1) * K_PASS, :].rearrange("(p t) c -> p t c", t=PACK),
-                    )
+                for g in range(max(1, r * ROUND_PASSES), (r + 1) * ROUND_PASSES):
+                    load_dq(g)
             qr_rows = W_qr.rearrange("(t p) c -> p t c", p=P)
             uq_rows = W_uq.rearrange("(t p) c -> p t c", p=P)
             nc.sync.dma_start(out=u_rows[0][:, :, 0:ROT_COLS], in_=qr_rows)
@@ -171,9 +182,6 @@ def tile_mla_pa_kernel(tc, h, W_dq, b_dq, W_uq, b_uq, W_qr, b_qr, out):
                 start_col = j * chunk_cols - ROT_COLS
                 nc.sync.dma_start(out=u_rows[j][:], in_=uq_rows[:, :, start_col : start_col + chunk_cols])
 
-            identity = consts.tile([P, P], F32)
-            masks.make_identity(nc, identity[:])
-            rot_cos, rot_sin = rotary_tables(nc, consts)
             b_dq_col = consts.tile([P, KV_TILES], F32)
 
             turned, h_grouped, dq_grouped = {}, {}, {}
@@ -189,12 +197,12 @@ def tile_mla_pa_kernel(tc, h, W_dq, b_dq, W_uq, b_uq, W_qr, b_qr, out):
                         )
 
             def group_first(g):
+                dq_grouped[g] = regroup(nc, w_stage, dq_rows[g][:], DQ_SCALAR_COLS)
                 h_grouped[g] = h_stage.tile([P, TOKENS * PACK], BF16, align_bytes=64, name="h_grouped")
                 nc.scalar.copy(
                     out=h_grouped[g][:].bitcast(F32).rearrange("p (s u) -> p s u", u=2),
                     in_=turned[g][:].rearrange("p u s -> p s u"),
                 )
-                dq_grouped[g] = regroup(nc, w_stage, dq_rows[g][:], DQ_SCALAR_COLS)
 
             def multiply_first(g):
                 nc.vector.quantize_mx(
@@ -259,11 +267,11 @@ def tile_mla_pa_kernel(tc, h, W_dq, b_dq, W_uq, b_uq, W_qr, b_qr, out):
             def spread_bias(pair):
                 spread = banks.tile([P, 2 * GROUP], BF16, tag="bank")
                 for i in range(2):
-                    start_col = (2 * pair + i) * GROUP
+                    n = 2 * pair + i
                     nc.tensor.matmul(
                         out=spread[:, i * GROUP : (i + 1) * GROUP],
-                        lhsT=ones[:],
-                        rhs=bias_row[:, start_col : start_col + GROUP],
+                        lhsT=identity_bf[:, n : n + 1].to_broadcast([P, P]),
+                        rhs=bias_rows[:],
                         start=True,
                         stop=True,
                     )

@@ -25,17 +25,17 @@ ROT_SCALE = 40.0
 ROT_BASE = 10000.0
 
 TOKENS = BATCH * SEQ
-ROUND_PASSES = 2
-ROUNDS = D_MODEL // (ROUND_PASSES * K_PASS)
-DQ_PASSES = ROUNDS * ROUND_PASSES
+DQ_PASSES = D_MODEL // K_PASS
+H_PASSES = (2, 4, 4)
+H_STARTS = (0, 2, 6)
 KV_TILES = D_KV // P
 
 ROT_COLS = HEADS * D_ROPE
 U_COLS = ROT_COLS + HEADS * SPLIT
 GROUP = 512
 GROUPS = U_COLS // GROUP
-CHUNK_GROUPS = 2
-CHUNKS = GROUPS // CHUNK_GROUPS
+CHUNK_GROUPS = (2, 4, 4)
+CHUNK_STARTS = (0, 2, 6)
 
 RUN = 8
 DQ_SCALAR_COLS = 224
@@ -131,12 +131,16 @@ def tile_mla_pa_kernel(tc, h, W_dq, b_dq, W_uq, b_uq, W_qr, b_qr, out):
         bias = keep.tile([P, U_COLS], BF16)
         u_codes = keep.tile([P, GROUPS, GROUP], U32, align_bytes=64)
         u_scales = keep.tile([P, GROUPS, GROUP], U8, align_bytes=64)
-        chunk_cols = CHUNK_GROUPS * GROUP
-        u_rows = [keep.tile([P, PACK, chunk_cols], BF16, name="u_rows%d" % j) for j in range(CHUNKS)]
+        u_rows = [
+            keep.tile([P, PACK, count * GROUP], BF16, name="u_rows%d" % start)
+            for start, count in zip(CHUNK_STARTS, CHUNK_GROUPS)
+        ]
 
         with tc.tile_pool(name="first", bufs=1) as first:
-            round_k = ROUND_PASSES * K_PASS
-            h_rows = [first.tile([P, BATCH, round_k], BF16, name="h_rows%d" % r) for r in range(ROUNDS)]
+            h_rows = {
+                start: first.tile([P, BATCH, count * K_PASS], BF16, name="h_rows%d" % start)
+                for start, count in zip(H_STARTS, H_PASSES)
+            }
             dq_rows = [first.tile([P, PACK, D_KV], BF16, name="dq_rows%d" % g) for g in range(DQ_PASSES)]
             h_codes = first.tile([P, DQ_PASSES, TOKENS], U32, align_bytes=64)
             h_scales = first.tile([P, DQ_PASSES, TOKENS], U8, align_bytes=64)
@@ -168,27 +172,31 @@ def tile_mla_pa_kernel(tc, h, W_dq, b_dq, W_uq, b_uq, W_qr, b_qr, out):
                     in_=W_dq[g * K_PASS : (g + 1) * K_PASS, :].rearrange("(p t) c -> p t c", t=PACK),
                 )
 
-            load_dq(0)
-            for r in range(ROUNDS):
-                k_range = slice(r * round_k, (r + 1) * round_k)
-                nc.sync.dma_start(out=h_rows[r][:], in_=h[:, :, k_range].rearrange("b s k -> s b k"))
-                for g in range(max(1, r * ROUND_PASSES), (r + 1) * ROUND_PASSES):
-                    load_dq(g)
+            for g in range(DQ_PASSES):
+                load_dq(g)
+                if g in h_rows:
+                    k_range = slice(g * K_PASS, g * K_PASS + h_rows[g].shape[2])
+                    nc.sync.dma_start(out=h_rows[g][:], in_=h[:, :, k_range].rearrange("b s k -> s b k"))
             qr_rows = W_qr.rearrange("(t p) c -> p t c", p=P)
             uq_rows = W_uq.rearrange("(t p) c -> p t c", p=P)
-            nc.sync.dma_start(out=u_rows[0][:, :, 0:ROT_COLS], in_=qr_rows)
-            nc.sync.dma_start(out=u_rows[0][:, :, ROT_COLS:chunk_cols], in_=uq_rows[:, :, 0 : chunk_cols - ROT_COLS])
-            for j in range(1, CHUNKS):
-                start_col = j * chunk_cols - ROT_COLS
-                nc.sync.dma_start(out=u_rows[j][:], in_=uq_rows[:, :, start_col : start_col + chunk_cols])
+            for start, count, chunk in zip(CHUNK_STARTS, CHUNK_GROUPS, u_rows):
+                first_col = start * GROUP - ROT_COLS
+                skip = 0
+                if start == 0:
+                    nc.sync.dma_start(out=chunk[:, :, 0:ROT_COLS], in_=qr_rows)
+                    skip = ROT_COLS
+                nc.sync.dma_start(
+                    out=chunk[:, :, skip:], in_=uq_rows[:, :, first_col + skip : first_col + count * GROUP]
+                )
 
             b_dq_col = consts.tile([P, KV_TILES], F32)
 
             turned, h_grouped, dq_grouped = {}, {}, {}
 
             def turn(g):
-                r, i = divmod(g, ROUND_PASSES)
-                words = h_rows[r][:].bitcast(F32).rearrange("s b (g p u) -> s b g u p", p=P, u=2)
+                start = [c for c in H_STARTS if c <= g][-1]
+                i = g - start
+                words = h_rows[start][:].bitcast(F32).rearrange("s b (g p u) -> s b g u p", p=P, u=2)
                 turned[g] = banks.tile([P, 2, TOKENS], F32, tag="bank", name="turned")
                 for b in range(BATCH):
                     for u in range(2):
@@ -238,8 +246,8 @@ def tile_mla_pa_kernel(tc, h, W_dq, b_dq, W_uq, b_uq, W_qr, b_qr, out):
             u_grouped, product = {}, {}
 
             def group_second(n):
-                j, i = divmod(n, CHUNK_GROUPS)
-                u_cols = u_rows[j][:, :, i * GROUP : (i + 1) * GROUP]
+                chunk, start = [(tile, c) for tile, c in zip(u_rows, CHUNK_STARTS) if c <= n][-1]
+                u_cols = chunk[:, :, (n - start) * GROUP : (n - start + 1) * GROUP]
                 if n >= GPSIMD_FROM:
                     u_grouped[n] = regroup(nc, w_stage, u_cols, GROUP - U_GPSIMD_COLS, gpsimd=True)
                 else:

from contextlib import ExitStack

import concourse.masks as masks
import concourse.mybir as mybir

F32 = mybir.dt.float32
BF16 = mybir.dt.bfloat16
I32 = mybir.dt.int32
U32 = mybir.dt.uint32
U8 = mybir.dt.uint8
FP8X4 = mybir.dt.float8_e4m3fn_x4
ACT = mybir.ActivationFunctionType
ALU = mybir.AluOpType

P = 128
PACK = 4
K_PASS = P * PACK

BATCH, SEQ, D_MODEL, HEADS, D_KV, D_ROPE = 2, 128, 5120, 8, 512, 16
D_HEAD = D_MODEL // HEADS
SPLIT = D_HEAD - D_ROPE
ROTATED = D_ROPE // 2
PAIRS = ROTATED // 2
ROT_SCALE = 40.0
ROT_BASE = 10000.0

TOKENS = BATCH * SEQ
DQ_PASSES = D_MODEL // K_PASS
H_PASSES = (2, 4, 4)
H_STARTS = (0, 2, 6)
KV_TILES = D_KV // P

ROT_COLS = HEADS * D_ROPE
U_COLS = ROT_COLS + HEADS * SPLIT
GROUP = 512
GROUPS = U_COLS // GROUP
CHUNK_GROUPS = (2, 4, 4)
CHUNK_STARTS = (0, 2, 6)

RUN = 8
DQ_SCALAR_COLS = 224
U_SCALAR_COLS = 432
GPSIMD_FROM = W_STAGE_BUFS = 4
U_GPSIMD_COLS = 128

TURN_AHEAD = 2

FLOPS = 2 * TOKENS * D_MODEL * D_KV + 2 * TOKENS * D_KV * U_COLS


def regroup(nc, pool, rows, scalar_cols, gpsimd=False):
    grouped = pool.tile([P, GROUP, PACK], BF16, align_bytes=64)
    src = rows.rearrange("p t (c i) -> p c t i", i=RUN)
    dst = grouped[:].rearrange("p (c i) t -> p c t i", i=RUN)
    cut = scalar_cols // RUN
    nc.scalar.copy(out=dst[:, 0:cut], in_=src[:, 0:cut])
    if gpsimd:
        nc.gpsimd.tensor_scalar(
            out=grouped[:, scalar_cols:, :], in0=rows[:, :, scalar_cols:].rearrange("p t c -> p c t"),
            scalar1=1.0, scalar2=0.0, op0=ALU.mult, op1=ALU.add,
        )
    else:
        nc.vector.tensor_copy(out=dst[:, cut:], in_=src[:, cut:])
    return grouped


def rotary_tables(nc, consts):
    position_int = consts.tile([P, 1], I32)
    nc.gpsimd.iota(position_int[:], pattern=[[0, 1]], base=0, channel_multiplier=1)
    position = consts.tile([P, 1], F32)
    nc.vector.tensor_copy(out=position[:], in_=position_int[:])

    sin_half = consts.tile([P, PAIRS], F32)
    sin_quarter = consts.tile([P, PAIRS], F32)
    for j in range(PAIRS):
        rate = 1.0 / (ROT_SCALE * ROT_BASE ** (j / PAIRS))
        nc.scalar.activation(out=sin_half[:, j : j + 1], in_=position[:], func=ACT.Sin, scale=rate / 2)
        nc.scalar.activation(out=sin_quarter[:, j : j + 1], in_=position[:], func=ACT.Sin, scale=rate / 4)

    cos_half = consts.tile([P, PAIRS], F32)
    nc.vector.tensor_tensor(out=cos_half[:], in0=sin_quarter[:], in1=sin_quarter[:], op=ALU.mult)
    nc.vector.tensor_scalar(out=cos_half[:], in0=cos_half[:], scalar1=-2.0, scalar2=1.0, op0=ALU.mult, op1=ALU.add)
    half_sin = consts.tile([P, PAIRS], F32)
    nc.vector.tensor_tensor(out=half_sin[:], in0=sin_half[:], in1=cos_half[:], op=ALU.mult)
    squared = consts.tile([P, PAIRS], F32)
    nc.vector.tensor_tensor(out=squared[:], in0=sin_half[:], in1=sin_half[:], op=ALU.mult)

    rot_cos = consts.tile([P, ROTATED], F32)
    rot_sin = consts.tile([P, ROTATED], F32)
    for half, sign in ((0, -2.0), (1, 2.0)):
        cols = slice(half * PAIRS, (half + 1) * PAIRS)
        nc.vector.tensor_scalar(out=rot_cos[:, cols], in0=squared[:], scalar1=-2.0, scalar2=1.0, op0=ALU.mult, op1=ALU.add)
        nc.vector.tensor_scalar_mul(out=rot_sin[:, cols], in0=half_sin[:], scalar1=sign)
    return rot_cos, rot_sin


def rotate(nc, pool, q_rots, rot_cos, rot_sin):
    low, high = slice(0, PAIRS), slice(PAIRS, ROTATED)
    straight = [pool.tile([P, HEADS, ROTATED], F32, name="straight%d" % b) for b in range(BATCH)]
    crossed = [pool.tile([P, HEADS, ROTATED], F32, name="crossed%d" % b) for b in range(BATCH)]
    for b in range(BATCH):
        nc.vector.tensor_tensor(
            out=straight[b][:], in0=q_rots[b][:, :, 0:ROTATED],
            in1=rot_cos[:].unsqueeze(1).to_broadcast([P, HEADS, ROTATED]), op=ALU.mult,
        )
    for here, there in ((low, high), (high, low)):
        for b in range(BATCH):
            nc.vector.tensor_tensor(
                out=crossed[b][:, :, here], in0=q_rots[b][:, :, there],
                in1=rot_sin[:, here].unsqueeze(1).to_broadcast([P, HEADS, PAIRS]), op=ALU.mult,
            )
    for b in range(BATCH):
        nc.vector.tensor_tensor(
            out=q_rots[b][:, :, 0:ROTATED], in0=straight[b][:], in1=crossed[b][:], op=ALU.add
        )


def tile_mla_pa_kernel(tc, h, W_dq, b_dq, W_uq, b_uq, W_qr, b_qr, out):
    nc = tc.nc
    with ExitStack() as ctx:
        ctx.enter_context(tc.manual_schedule())
        consts = ctx.enter_context(tc.tile_pool(name="consts", bufs=1))
        keep = ctx.enter_context(tc.tile_pool(name="keep", bufs=1))
        h_stage = ctx.enter_context(tc.tile_pool(name="h_stage", bufs=3))
        w_stage = ctx.enter_context(tc.tile_pool(name="w_stage", bufs=W_STAGE_BUFS))
        accs = ctx.enter_context(tc.psum_pool(name="accs", bufs=1))
        banks = ctx.enter_context(tc.psum_pool(name="banks", bufs=4))

        cq_codes = keep.tile([P, TOKENS], U32, align_bytes=64)
        cq_scales = keep.tile([P, TOKENS], U8, align_bytes=64)
        bias = keep.tile([P, U_COLS], BF16)
        u_codes = keep.tile([P, GROUPS, GROUP], U32, align_bytes=64)
        u_scales = keep.tile([P, GROUPS, GROUP], U8, align_bytes=64)
        u_rows = [
            keep.tile([P, PACK, count * GROUP], BF16, name="u_rows%d" % start)
            for start, count in zip(CHUNK_STARTS, CHUNK_GROUPS)
        ]

        with tc.tile_pool(name="first", bufs=1) as first:
            h_rows = {
                start: first.tile([P, BATCH, count * K_PASS], BF16, name="h_rows%d" % start)
                for start, count in zip(H_STARTS, H_PASSES)
            }
            dq_rows = [first.tile([P, PACK, D_KV], BF16, name="dq_rows%d" % g) for g in range(DQ_PASSES)]
            h_codes = first.tile([P, DQ_PASSES, TOKENS], U32, align_bytes=64)
            h_scales = first.tile([P, DQ_PASSES, TOKENS], U8, align_bytes=64)
            dq_codes = first.tile([P, DQ_PASSES, D_KV], U32, align_bytes=64)
            dq_scales = first.tile([P, DQ_PASSES, D_KV], U8, align_bytes=64)
            acc = [accs.tile([P, TOKENS], F32, name="acc%d" % m) for m in range(KV_TILES)]

            bias_rows = first.tile([P, GROUP], BF16)
            nc.vector.memset(bias_rows[:].bitcast(I32), 0)
            rot_cos, rot_sin = rotary_tables(nc, consts)
            identity = consts.tile([P, P], F32)
            masks.make_identity(nc, identity[:])
            identity_bf = consts.tile([P, P], BF16)
            masks.make_identity(nc, identity_bf[:])
            first_cols = GROUP - ROT_COLS
            nc.gpsimd.dma_start(out=bias_rows[0:1, 0:ROT_COLS], in_=b_qr.unsqueeze(0))
            nc.gpsimd.dma_start(out=bias_rows[0:1, ROT_COLS:GROUP], in_=b_uq[0:first_cols].unsqueeze(0))
            nc.gpsimd.dma_start(
                out=bias_rows[1:GROUPS, :], in_=b_uq[first_cols:].rearrange("(n c) -> n c", c=GROUP)
            )

            b_dq_bf = consts.tile([P, KV_TILES], BF16)
            with nc.allow_non_contiguous_dma(reason="512 bias values, one to a partition and tile"):
                nc.gpsimd.dma_start(out=b_dq_bf[:], in_=b_dq.rearrange("(m p) -> p m", p=P))

            def load_dq(g):
                nc.sync.dma_start(
                    out=dq_rows[g][:],
                    in_=W_dq[g * K_PASS : (g + 1) * K_PASS, :].rearrange("(p t) c -> p t c", t=PACK),
                )

            for g in range(DQ_PASSES):
                load_dq(g)
                if g in h_rows:
                    k_range = slice(g * K_PASS, g * K_PASS + h_rows[g].shape[2])
                    nc.sync.dma_start(out=h_rows[g][:], in_=h[:, :, k_range].rearrange("b s k -> s b k"))
            qr_rows = W_qr.rearrange("(t p) c -> p t c", p=P)
            uq_rows = W_uq.rearrange("(t p) c -> p t c", p=P)
            for start, count, chunk in zip(CHUNK_STARTS, CHUNK_GROUPS, u_rows):
                first_col = start * GROUP - ROT_COLS
                skip = 0
                if start == 0:
                    nc.sync.dma_start(out=chunk[:, :, 0:ROT_COLS], in_=qr_rows)
                    skip = ROT_COLS
                nc.sync.dma_start(
                    out=chunk[:, :, skip:], in_=uq_rows[:, :, first_col + skip : first_col + count * GROUP]
                )

            b_dq_col = consts.tile([P, KV_TILES], F32)

            turned, h_grouped, dq_grouped = {}, {}, {}

            def turn(g):
                start = [c for c in H_STARTS if c <= g][-1]
                i = g - start
                words = h_rows[start][:].bitcast(F32).rearrange("s b (g p u) -> s b g u p", p=P, u=2)
                turned[g] = banks.tile([P, 2, TOKENS], F32, tag="bank", name="turned")
                for b in range(BATCH):
                    for u in range(2):
                        nc.tensor.transpose(
                            out=turned[g][:, u, b * SEQ : (b + 1) * SEQ], in_=words[:, b, i, u, :], identity=identity[:]
                        )

            def group_first(g):
                dq_grouped[g] = regroup(nc, w_stage, dq_rows[g][:], DQ_SCALAR_COLS)
                h_grouped[g] = h_stage.tile([P, TOKENS * PACK], BF16, align_bytes=64, name="h_grouped")
                nc.scalar.copy(
                    out=h_grouped[g][:].bitcast(F32).rearrange("p (s u) -> p s u", u=2),
                    in_=turned[g][:].rearrange("p u s -> p s u"),
                )

            def multiply_first(g):
                nc.vector.quantize_mx(
                    out=h_codes[:, g, :].bitcast(FP8X4), scales=h_scales[:, g, :], in_=h_grouped[g][:]
                )
                nc.vector.quantize_mx(
                    out=dq_codes[:, g, :].bitcast(FP8X4),
                    scales=dq_scales[:, g, :],
                    in_=dq_grouped[g][:].rearrange("p c t -> p (c t)"),
                )
                for m in range(KV_TILES):
                    cols = slice(m * P, (m + 1) * P)
                    nc.tensor.matmul_mx(
                        out=acc[m][:],
                        lhsT=dq_codes[:, g, cols].bitcast(FP8X4),
                        lhsT_scale=dq_scales[:, g, cols],
                        rhs=h_codes[:, g, :].bitcast(FP8X4),
                        rhs_scale=h_scales[:, g, :],
                        start=(g == 0),
                        stop=(g == DQ_PASSES - 1),
                    )

            for g in range(TURN_AHEAD):
                turn(g)
            for step in range(DQ_PASSES + 1):
                if step + TURN_AHEAD < DQ_PASSES:
                    turn(step + TURN_AHEAD)
                if step < DQ_PASSES:
                    group_first(step)
                if step >= 1:
                    multiply_first(step - 1)

            u_grouped, product = {}, {}

            def group_second(n):
                chunk, start = [(tile, c) for tile, c in zip(u_rows, CHUNK_STARTS) if c <= n][-1]
                u_cols = chunk[:, :, (n - start) * GROUP : (n - start + 1) * GROUP]
                if n >= GPSIMD_FROM:
                    u_grouped[n] = regroup(nc, w_stage, u_cols, GROUP - U_GPSIMD_COLS, gpsimd=True)
                else:
                    u_grouped[n] = regroup(nc, w_stage, u_cols, U_SCALAR_COLS)

            def multiply_second(n):
                nc.vector.quantize_mx(
                    out=u_codes[:, n, :].bitcast(FP8X4),
                    scales=u_scales[:, n, :],
                    in_=u_grouped[n][:].rearrange("p c t -> p (c t)"),
                )
                for b in range(BATCH):
                    tokens = slice(b * SEQ, (b + 1) * SEQ)
                    product[n, b] = banks.tile([P, GROUP], F32, tag="bank", name="product")
                    nc.tensor.matmul_mx(
                        out=product[n, b][:],
                        lhsT=cq_codes[:, tokens].bitcast(FP8X4),
                        lhsT_scale=cq_scales[:, tokens],
                        rhs=u_codes[:, n, :].bitcast(FP8X4),
                        rhs_scale=u_scales[:, n, :],
                        start=True,
                        stop=True,
                    )

            def spread_bias(pair):
                spread = banks.tile([P, 2 * GROUP], BF16, tag="bank")
                for i in range(2):
                    n = 2 * pair + i
                    nc.tensor.matmul(
                        out=spread[:, i * GROUP : (i + 1) * GROUP],
                        lhsT=identity_bf[:, n : n + 1].to_broadcast([P, P]),
                        rhs=bias_rows[:],
                        start=True,
                        stop=True,
                    )
                cols = slice(2 * pair * GROUP, 2 * (pair + 1) * GROUP)
                if pair % 2 == 0:
                    nc.scalar.copy(out=bias[:, cols], in_=spread[:])
                else:
                    nc.vector.tensor_copy(out=bias[:, cols], in_=spread[:])

            group_second(0)
            nc.vector.tensor_copy(out=b_dq_col[:], in_=b_dq_bf[:])
            cq_rows = first.tile([P, KV_TILES, TOKENS], BF16)
            for m in range(KV_TILES):
                if m % 2 == 0:
                    nc.scalar.activation(
                        out=cq_rows[:, m, :], in_=acc[m][:], func=ACT.Identity, bias=b_dq_col[:, m : m + 1]
                    )
                else:
                    nc.vector.tensor_scalar_add(
                        out=cq_rows[:, m, :], in0=acc[m][:], scalar1=b_dq_col[:, m : m + 1]
                    )
            spread_bias(0)
            spread_bias(1)
            cq_grouped = first.tile([P, TOKENS, PACK], BF16, align_bytes=64)
            nc.vector.tensor_copy(
                out=cq_grouped[:].rearrange("p (c i) t -> p c t i", i=RUN),
                in_=cq_rows[:].rearrange("p t (c i) -> p c t i", i=RUN),
            )
            group_second(1)
            nc.vector.quantize_mx(
                out=cq_codes[:].bitcast(FP8X4),
                scales=cq_scales[:],
                in_=cq_grouped[:].rearrange("p c t -> p (c t)"),
            )
            for pair in range(2, GROUPS // 2):
                spread_bias(pair)
            multiply_second(0)

        results = ctx.enter_context(tc.tile_pool(name="results", bufs=1))
        result = [results.tile([P, U_COLS], F32, name="result%d" % b) for b in range(BATCH)]

        def leave_second(n):
            cols = slice(n * GROUP, (n + 1) * GROUP)
            for b in range(BATCH):
                nc.vector.tensor_tensor(out=result[b][:, cols], in0=product[n, b][:], in1=bias[:, cols], op=ALU.add)
            if n == 0:
                q_rots = [result[b][:, 0:ROT_COLS].rearrange("p (a d) -> p a d", d=D_ROPE) for b in range(BATCH)]
                rotate(nc, results, q_rots, rot_cos, rot_sin)
                for b in range(BATCH):
                    nc.sync.dma_start(out=out[b, :, :, SPLIT:D_HEAD], in_=q_rots[b])
            for a in range(HEADS):
                start_col = ROT_COLS + a * SPLIT
                if (start_col + SPLIT - 1) // GROUP == n:
                    for b in range(BATCH):
                        nc.sync.dma_start(out=out[b, :, a, 0:SPLIT], in_=result[b][:, start_col : start_col + SPLIT])

        for step in range(2, GROUPS + 2):
            if step < GROUPS:
                group_second(step)
            if step - 1 < GROUPS:
                multiply_second(step - 1)
            leave_second(step - 2)
